import numpy as np
import ml_dtypes


def mxq(x, axis, fmt="e4m3"):
    dtype, down = {"e4m3": (ml_dtypes.float8_e4m3fn, 7), "e5m2": (ml_dtypes.float8_e5m2, 14)}[fmt]
    v = np.moveaxis(np.asarray(x, np.float32).astype(ml_dtypes.bfloat16).astype(np.float64), axis, -1)
    blocks = v.reshape(v.shape[:-1] + (-1, 32))
    amax = np.abs(blocks).max(-1, keepdims=True)
    byte = np.maximum(np.where(amax > 0, np.frexp(amax)[1] - 1 + 127, 0) - down, 1)
    scale = np.exp2(byte - 127.0)
    codes = (blocks / scale).astype(np.float32).astype(dtype).astype(np.float64)
    return np.moveaxis((codes * scale).reshape(v.shape), -1, axis)


WIDE = False


def mx_kscale(k):
    if not WIDE:
        return np.ones(k)
    levels = np.array([10, -10, 5, -5, 0])
    a = np.random.permutation(np.resize(levels, k // 512 * 4)).reshape(k // 512, 4)
    idx = np.arange(k)
    return np.exp2(a[idx // 512, idx % 128 // 32])


BF16 = ml_dtypes.bfloat16


def bf(x):
    return np.asarray(x, np.float32).astype(BF16)


def f64(x):
    return np.asarray(x).astype(np.float64)


E2M1 = np.array([0.0, 0.5, 1.0, 1.5, 2.0, 3.0, 4.0, 6.0, -0.0, -0.5, -1.0, -1.5, -2.0, -3.0, -4.0, -6.0])


def pack_weight(w, fmt):
    k, n = w.shape
    w = f64(bf(w)).reshape(k // 32, 32, n)
    amax = np.abs(w).max(1)
    if fmt == "e4m3":
        byte = np.frexp(amax)[1] - 1 + 127 - 7
    else:
        mant, ex = np.frexp(amax / 6.0)
        byte = np.where(mant > 0.5, ex, ex - 1) + 127
    byte = np.clip(np.where(amax > 0, byte, 1), 1, 254)
    scaled = (w * np.exp2(127.0 - byte)[:, None, :]).reshape(k, n).astype(np.float32)
    by_word = np.ascontiguousarray(scaled.reshape(k // 512, 128, 4, n).transpose(0, 1, 3, 2))
    if fmt == "e4m3":
        words = by_word.astype(ml_dtypes.float8_e4m3fn).view(np.uint8)
    else:
        c = by_word.astype(ml_dtypes.float4_e2m1fn).view(np.uint8) & 0xF
        words = c[..., 0::2] | (c[..., 1::2] << 4)
    return np.ascontiguousarray(words), np.ascontiguousarray(byte.astype(np.uint8).reshape(k // 512, 16, n))


def unpack_weight(words, scales, fmt):
    g, p, n, _ = words.shape
    if fmt == "e4m3":
        vals = np.ascontiguousarray(words).view(ml_dtypes.float8_e4m3fn).astype(np.float64)
    else:
        nib = np.empty((g, p, n, 4), np.uint8)
        nib[..., 0::2] = words & 0xF
        nib[..., 1::2] = words >> 4
        vals = E2M1[nib]
    vals = vals * np.repeat(np.exp2(scales.astype(np.float64) - 127.0), 8, axis=1)[..., None]
    return vals.transpose(0, 1, 3, 2).reshape(g * 512, n)


B, X, N, OS = 128, 16384, 1536, 512
H = N - OS


def setup_inputs():
    s, t = mx_kscale(X), mx_kscale(H)
    std0 = np.sqrt(2.0 / X)
    std1 = np.sqrt(2.0 / (X + H))
    row_scale = np.concatenate([std0 * t, np.full(OS, std1)])
    bias_scale = np.concatenate([t, np.ones(OS)])
    x = bf(np.random.standard_normal((B, X)) * s)
    w0_words, w0_scales = pack_weight((np.random.standard_normal((N, X)) * row_scale[:, None] / s).T, "e4m3")
    w1_words, w1_scales = pack_weight((np.random.standard_normal((OS, H)) * std1 / t).T, "e4m3")
    biases = bf(np.random.random(N) * bias_scale)
    return {"x": x,
            "w0_words": w0_words, "w0_scales": w0_scales,
            "w1_words": w1_words, "w1_scales": w1_scales,
            "biases": biases}


def reference(x, w0_words, w0_scales, w1_words, w1_scales, biases):
    n = w0_words.shape[2]
    os_ = w1_words.shape[2]
    z = (mxq(f64(x), 1, "e4m3") @ unpack_weight(w0_words, w0_scales, "e4m3")) + f64(biases)
    h = np.maximum(z[:, : n - os_], 0.0)
    return z[:, n - os_:] + (mxq(h, 1, "e4m3") @ unpack_weight(w1_words, w1_scales, "e4m3"))

@@ -1,0 +1,210 @@
+from contextlib import ExitStack
+
+import concourse.mybir as mybir
+from concourse.masks import make_identity
+
+F32 = mybir.dt.float32
+BF16 = mybir.dt.bfloat16
+I32 = mybir.dt.int32
+U32 = mybir.dt.uint32
+U8 = mybir.dt.uint8
+FP8X4 = mybir.dt.float8_e4m3fn_x4
+ADD = mybir.AluOpType.add
+
+P = 128
+PACK = 4
+K_PASS = P * PACK
+N_TILE = 512
+
+BATCH = 128
+INPUTS = 16384
+NODES = 1536
+HIDDEN = 1024
+OUT_NODES = NODES - HIDDEN
+GROUPS = INPUTS // K_PASS
+HIDDEN_GROUPS = HIDDEN // K_PASS
+OUT_BANK = HIDDEN_GROUPS
+
+QUADRANTS = 4
+PLANES_PER_TILE = 4
+
+X_CHUNK_GROUPS = 8
+X_CHUNK = X_CHUNK_GROUPS * K_PASS
+X_CHUNKS = GROUPS // X_CHUNK_GROUPS
+
+SPLIT_GROUPS = 12
+WHOLE_GROUPS = GROUPS - SPLIT_GROUPS
+
+FLOPS = 2 * BATCH * INPUTS * NODES + 2 * BATCH * HIDDEN * OUT_NODES
+
+
+def load_scale_planes(nc, planes, scales):
+    rows = PACK * scales.shape[0]
+    for quadrant in range(QUADRANTS):
+        nc.gpsimd.dma_start(
+            out=planes[32 * quadrant : 32 * quadrant + rows, :].bitcast(F32),
+            in_=scales[:, 4 * quadrant : 4 * quadrant + 4, :].bitcast(F32),
+        )
+
+
+def tile_spn_k_kernel(tc, x, w0_words, w0_scales, w1_words, w1_scales, biases, out):
+    nc = tc.nc
+    with ExitStack() as ctx:
+        ctx.enter_context(tc.manual_schedule())
+        keep = ctx.enter_context(tc.tile_pool(name="keep", bufs=1))
+        x_pool = ctx.enter_context(tc.tile_pool(name="x", bufs=X_CHUNKS))
+        stage = ctx.enter_context(tc.tile_pool(name="stage", bufs=2))
+        whole_pool = ctx.enter_context(tc.tile_pool(name="whole", bufs=10))
+        hidden_pool = ctx.enter_context(tc.tile_pool(name="hidden", bufs=6))
+        out_pool = ctx.enter_context(tc.tile_pool(name="outcols", bufs=SPLIT_GROUPS))
+        acc_pool = ctx.enter_context(tc.psum_pool(name="acc", bufs=1))
+        work = ctx.enter_context(tc.psum_pool(name="work", bufs=4))
+
+        ident_f32 = keep.tile([P, P], F32)
+        make_identity(nc, ident_f32[:])
+        ident_bf16 = keep.tile([P, P], BF16)
+        make_identity(nc, ident_bf16[:])
+
+        bias_rows = keep.tile([P, NODES], BF16)
+        nc.vector.memset(bias_rows[:], 0.0)
+        nc.scalar.dma_start(out=bias_rows[0:1, :], in_=biases.unsqueeze(0))
+        ones = keep.tile([P, P], BF16)
+        nc.vector.memset(ones[:], 1.0)
+
+        w0_planes = keep.tile([P, GROUPS // PLANES_PER_TILE, NODES], U8, align_bytes=64)
+        nc.vector.memset(w0_planes[:].bitcast(I32), 0)
+        w1_planes = keep.tile([P, OUT_NODES], U8, align_bytes=64)
+        nc.vector.memset(w1_planes[:].bitcast(I32), 0)
+
+        x_chunks = []
+        for c in range(X_CHUNKS):
+            x_chunk = x_pool.tile([P, X_CHUNK], BF16, name="x_chunk")
+            nc.sync.dma_start(out=x_chunk[:], in_=x[:, c * X_CHUNK : (c + 1) * X_CHUNK])
+            x_chunks.append(x_chunk)
+
+        w1_sb = keep.tile([P, HIDDEN_GROUPS, OUT_NODES], U32, align_bytes=64)
+        nc.sync.dma_start(
+            out=w1_sb[:].bitcast(I32),
+            in_=w1_words.rearrange("g p n t -> p g (n t)").bitcast(I32),
+        )
+
+        for c in range(GROUPS // PLANES_PER_TILE):
+            load_scale_planes(
+                nc, w0_planes[:, c, :], w0_scales[c * PLANES_PER_TILE : (c + 1) * PLANES_PER_TILE]
+            )
+        load_scale_planes(nc, w1_planes[:], w1_scales)
+
+        x_codes = keep.tile([P, GROUPS, BATCH], U32, align_bytes=64)
+        x_planes = keep.tile([P, GROUPS, BATCH], U8, align_bytes=64)
+        for c in range(X_CHUNKS):
+            x_words = x_chunks[c][:].bitcast(F32).rearrange("b (g p u) -> b g p u", p=P, u=2)
+            grouped = stage.tile([P, X_CHUNK], BF16, align_bytes=64)
+            grouped_words = grouped[:].bitcast(F32).rearrange("p (g b u) -> p g b u", b=BATCH, u=2)
+            for first in range(0, X_CHUNK_GROUPS, 2):
+                xt = work.tile([P, 2, 2, BATCH], F32, tag="work")
+                for g in range(2):
+                    for u in range(2):
+                        nc.tensor.transpose(xt[:, g, u, :], x_words[:, first + g, :, u], ident_f32[:])
+                nc.scalar.copy(
+                    out=grouped_words[:, first : first + 2],
+                    in_=xt[:].rearrange("p g u b -> p g b u"),
+                )
+            groups = slice(c * X_CHUNK_GROUPS, (c + 1) * X_CHUNK_GROUPS)
+            nc.vector.quantize_mx(
+                out=x_codes[:, groups, :].rearrange("p g b -> p (g b)").bitcast(FP8X4),
+                scales=x_planes[:, groups, :].rearrange("p g b -> p (g b)"),
+                in_=grouped[:],
+            )
+
+        bias_hidden = keep.tile([P, HIDDEN_GROUPS, PACK, P], F32)
+        bias_out = keep.tile([P, OUT_NODES], F32)
+        for n in range(NODES // N_TILE):
+            spread = work.tile([P, N_TILE], F32, tag="work")
+            nc.tensor.matmul(
+                spread[:], lhsT=ones[:], rhs=bias_rows[:, n * N_TILE : (n + 1) * N_TILE],
+                start=True, stop=True,
+            )
+            if n < HIDDEN_GROUPS:
+                nc.vector.tensor_copy(
+                    out=bias_hidden[:, n], in_=spread[:].rearrange("b (p t) -> b t p", t=PACK)
+                )
+            else:
+                nc.vector.tensor_copy(out=bias_out[:], in_=spread[:])
+
+        acc = [acc_pool.tile([P, N_TILE], F32, name="acc%d" % n) for n in range(NODES // N_TILE)]
+
+        def load_w0(pool, g, first_node, nodes):
+            words = pool.tile([P, nodes], U32, name="words", align_bytes=64)
+            nc.sync.dma_start(
+                out=words[:].bitcast(I32),
+                in_=w0_words[g].rearrange("p n t -> p (n t)").bitcast(I32)[
+                    :, first_node : first_node + nodes
+                ],
+            )
+            return words
+
+        def first_stage_passes(g, words, banks, stop):
+            plane_tile, plane = divmod(g, PLANES_PER_TILE)
+            for i, n in enumerate(banks):
+                nc.tensor.matmul_mx(
+                    out=acc[n][:],
+                    lhsT=x_codes[:, g, :].bitcast(FP8X4),
+                    lhsT_scale=x_planes[:, g, :],
+                    rhs=words[:, i * N_TILE : (i + 1) * N_TILE].bitcast(FP8X4),
+                    rhs_scale=w0_planes[PACK * plane : P, plane_tile, n * N_TILE : (n + 1) * N_TILE],
+                    start=(g == 0),
+                    stop=stop,
+                )
+
+        hidden_banks = list(range(HIDDEN_GROUPS))
+        for g in range(WHOLE_GROUPS):
+            words = load_w0(whole_pool, g, 0, NODES)
+            first_stage_passes(g, words, hidden_banks + [OUT_BANK], stop=False)
+        for g in range(WHOLE_GROUPS, GROUPS):
+            words = load_w0(hidden_pool, g, 0, HIDDEN)
+            first_stage_passes(g, words, hidden_banks, stop=(g == GROUPS - 1))
+        out_words = [load_w0(out_pool, g, HIDDEN, OUT_NODES) for g in range(WHOLE_GROUPS, GROUPS)]
+
+        h = keep.tile([P, HIDDEN_GROUPS, PACK, P], BF16)
+        z_hidden = keep.tile([P, HIDDEN_GROUPS, PACK, P], F32)
+        for g in range(HIDDEN_GROUPS):
+            nc.vector.tensor_tensor(
+                out=z_hidden[:, g],
+                in0=acc[g][:].rearrange("b (p t) -> b t p", t=PACK),
+                in1=bias_hidden[:, g],
+                op=ADD,
+            )
+        for g in range(HIDDEN_GROUPS):
+            nc.vector.tensor_scalar_max(out=h[:, g], in0=z_hidden[:, g], scalar1=0.0)
+
+        h_grouped = keep.tile([P, HIDDEN_GROUPS, BATCH, PACK], BF16, align_bytes=64)
+        h_codes = keep.tile([P, HIDDEN_GROUPS, BATCH], U32, align_bytes=64)
+        h_planes = keep.tile([P, HIDDEN_GROUPS, BATCH], U8, align_bytes=64)
+        for g in range(HIDDEN_GROUPS):
+            ht = work.tile([P, PACK, BATCH], BF16, tag="work")
+            for t in range(PACK):
+                nc.tensor.transpose(ht[:, t, :], h[:, g, t, :], ident_bf16[:])
+            nc.scalar.copy(out=h_grouped[:, g], in_=ht[:].rearrange("p t b -> p b t"))
+            nc.vector.quantize_mx(
+                out=h_codes[:, g, :].bitcast(FP8X4),
+                scales=h_planes[:, g, :],
+                in_=h_grouped[:, g].rearrange("p b t -> p (b t)"),
+            )
+
+        for g in range(WHOLE_GROUPS, GROUPS - 1):
+            first_stage_passes(g, out_words[g - WHOLE_GROUPS], [OUT_BANK], stop=False)
+        for g in range(HIDDEN_GROUPS):
+            nc.tensor.matmul_mx(
+                out=acc[OUT_BANK][:],
+                lhsT=h_codes[:, g, :].bitcast(FP8X4),
+                lhsT_scale=h_planes[:, g, :],
+                rhs=w1_sb[:, g, :].bitcast(FP8X4),
+                rhs_scale=w1_planes[PACK * g : P, :],
+                start=False,
+                stop=False,
+            )
+        first_stage_passes(GROUPS - 1, out_words[-1], [OUT_BANK], stop=True)
+
+        result = keep.tile([P, OUT_NODES], F32)
+        nc.vector.tensor_tensor(out=result[:], in0=acc[OUT_BANK][:], in1=bias_out[:], op=ADD)
+        nc.sync.dma_start(out=out[:, :], in_=result[:])

@@ -34,6 +34,7 @@ X_CHUNKS = GROUPS // X_CHUNK_GROUPS
 
 SPLIT_GROUPS = 12
 WHOLE_GROUPS = GROUPS - SPLIT_GROUPS
+OUT_PASSES_BEFORE_H = 4
 
 FLOPS = 2 * BATCH * INPUTS * NODES + 2 * BATCH * HIDDEN * OUT_NODES
 
@@ -177,6 +178,9 @@ def tile_spn_k_kernel(tc, x, w0_words, w0_scales, w1_words, w1_scales, biases, o
         for g in range(HIDDEN_GROUPS):
             nc.vector.tensor_scalar_max(out=h[:, g], in0=z_hidden[:, g], scalar1=0.0)
 
+        for g in range(WHOLE_GROUPS, WHOLE_GROUPS + OUT_PASSES_BEFORE_H):
+            first_stage_passes(g, out_words[g - WHOLE_GROUPS], [OUT_BANK], stop=False)
+
         h_grouped = keep.tile([P, HIDDEN_GROUPS, BATCH, PACK], BF16, align_bytes=64)
         h_codes = keep.tile([P, HIDDEN_GROUPS, BATCH], U32, align_bytes=64)
         h_planes = keep.tile([P, HIDDEN_GROUPS, BATCH], U8, align_bytes=64)
@@ -191,7 +195,7 @@ def tile_spn_k_kernel(tc, x, w0_words, w0_scales, w1_words, w1_scales, biases, o
                 in_=h_grouped[:, g].rearrange("p b t -> p (b t)"),
             )
 
-        for g in range(WHOLE_GROUPS, GROUPS - 1):
+        for g in range(WHOLE_GROUPS + OUT_PASSES_BEFORE_H, GROUPS - 1):
             first_stage_passes(g, out_words[g - WHOLE_GROUPS], [OUT_BANK], stop=False)
         for g in range(HIDDEN_GROUPS):
             nc.tensor.matmul_mx(

@@ -10,6 +10,7 @@ U32 = mybir.dt.uint32
 U8 = mybir.dt.uint8
 FP8X4 = mybir.dt.float8_e4m3fn_x4
 ADD = mybir.AluOpType.add
+RELU = mybir.ActivationFunctionType.Relu
 
 P = 128
 PACK = 4
@@ -23,7 +24,8 @@ HIDDEN = 1024
 OUT_NODES = NODES - HIDDEN
 GROUPS = INPUTS // K_PASS
 HIDDEN_GROUPS = HIDDEN // K_PASS
-OUT_BANK = HIDDEN_GROUPS
+OUT_HALF = OUT_NODES // 2
+OUT_BANKS = [HIDDEN_GROUPS, HIDDEN_GROUPS + 1]
 
 QUADRANTS = 4
 PLANES_PER_TILE = 4
@@ -32,9 +34,10 @@ X_CHUNK_GROUPS = 8
 X_CHUNK = X_CHUNK_GROUPS * K_PASS
 X_CHUNKS = GROUPS // X_CHUNK_GROUPS
 
-SPLIT_GROUPS = 12
+SPLIT_GROUPS = 8
 WHOLE_GROUPS = GROUPS - SPLIT_GROUPS
-OUT_PASSES_BEFORE_H = 4
+OUT_PASSES_BEFORE_H = 1
+OUT_PASSES_AFTER_H = 2
 
 FLOPS = 2 * BATCH * INPUTS * NODES + 2 * BATCH * HIDDEN * OUT_NODES
 
@@ -63,8 +66,6 @@ def tile_spn_k_kernel(tc, x, w0_words, w0_scales, w1_words, w1_scales, biases, o
 
         ident_f32 = keep.tile([P, P], F32)
         make_identity(nc, ident_f32[:])
-        ident_bf16 = keep.tile([P, P], BF16)
-        make_identity(nc, ident_bf16[:])
 
         bias_rows = keep.tile([P, NODES], BF16)
         nc.vector.memset(bias_rows[:], 0.0)
@@ -82,12 +83,6 @@ def tile_spn_k_kernel(tc, x, w0_words, w0_scales, w1_words, w1_scales, biases, o
             x_chunk = x_pool.tile([P, X_CHUNK], BF16, name="x_chunk")
             nc.sync.dma_start(out=x_chunk[:], in_=x[:, c * X_CHUNK : (c + 1) * X_CHUNK])
             x_chunks.append(x_chunk)
-
-        w1_sb = keep.tile([P, HIDDEN_GROUPS, OUT_NODES], U32, align_bytes=64)
-        nc.sync.dma_start(
-            out=w1_sb[:].bitcast(I32),
-            in_=w1_words.rearrange("g p n t -> p g (n t)").bitcast(I32),
-        )
 
         for c in range(GROUPS // PLANES_PER_TILE):
             load_scale_planes(
@@ -132,7 +127,11 @@ def tile_spn_k_kernel(tc, x, w0_words, w0_scales, w1_words, w1_scales, biases, o
             else:
                 nc.vector.tensor_copy(out=bias_out[:], in_=spread[:])
 
-        acc = [acc_pool.tile([P, N_TILE], F32, name="acc%d" % n) for n in range(NODES // N_TILE)]
+        acc_nodes = [(n * N_TILE, N_TILE) for n in range(HIDDEN_GROUPS)]
+        acc_nodes += [(HIDDEN + i * OUT_HALF, OUT_HALF) for i in range(2)]
+        acc = [
+            acc_pool.tile([P, nodes], F32, name="acc%d" % n) for n, (first, nodes) in enumerate(acc_nodes)
+        ]
 
         def load_w0(pool, g, first_node, nodes):
             words = pool.tile([P, nodes], U32, name="words", align_bytes=64)
@@ -145,14 +144,16 @@ def tile_spn_k_kernel(tc, x, w0_words, w0_scales, w1_words, w1_scales, biases, o
             return words
 
         def first_stage_passes(g, words, banks, stop):
+            first_word = acc_nodes[banks[0]][0]
             plane_tile, plane = divmod(g, PLANES_PER_TILE)
-            for i, n in enumerate(banks):
+            for n in banks:
+                first, nodes = acc_nodes[n]
                 nc.tensor.matmul_mx(
                     out=acc[n][:],
                     lhsT=x_codes[:, g, :].bitcast(FP8X4),
                     lhsT_scale=x_planes[:, g, :],
-                    rhs=words[:, i * N_TILE : (i + 1) * N_TILE].bitcast(FP8X4),
-                    rhs_scale=w0_planes[PACK * plane : P, plane_tile, n * N_TILE : (n + 1) * N_TILE],
+                    rhs=words[:, first - first_word : first - first_word + nodes].bitcast(FP8X4),
+                    rhs_scale=w0_planes[PACK * plane : P, plane_tile, first : first + nodes],
                     start=(g == 0),
                     stop=stop,
                 )
@@ -160,13 +161,17 @@ def tile_spn_k_kernel(tc, x, w0_words, w0_scales, w1_words, w1_scales, biases, o
         hidden_banks = list(range(HIDDEN_GROUPS))
         for g in range(WHOLE_GROUPS):
             words = load_w0(whole_pool, g, 0, NODES)
-            first_stage_passes(g, words, hidden_banks + [OUT_BANK], stop=False)
+            first_stage_passes(g, words, hidden_banks + OUT_BANKS, stop=False)
         for g in range(WHOLE_GROUPS, GROUPS):
             words = load_w0(hidden_pool, g, 0, HIDDEN)
             first_stage_passes(g, words, hidden_banks, stop=(g == GROUPS - 1))
+        w1_sb = keep.tile([P, HIDDEN_GROUPS, OUT_NODES], U32, align_bytes=64)
+        nc.sync.dma_start(
+            out=w1_sb[:].bitcast(I32),
+            in_=w1_words.rearrange("g p n t -> p g (n t)").bitcast(I32),
+        )
         out_words = [load_w0(out_pool, g, HIDDEN, OUT_NODES) for g in range(WHOLE_GROUPS, GROUPS)]
 
-        h = keep.tile([P, HIDDEN_GROUPS, PACK, P], BF16)
         z_hidden = keep.tile([P, HIDDEN_GROUPS, PACK, P], F32)
         for g in range(HIDDEN_GROUPS):
             nc.vector.tensor_tensor(
@@ -175,40 +180,47 @@ def tile_spn_k_kernel(tc, x, w0_words, w0_scales, w1_words, w1_scales, biases, o
                 in1=bias_hidden[:, g],
                 op=ADD,
             )
-        for g in range(HIDDEN_GROUPS):
-            nc.vector.tensor_scalar_max(out=h[:, g], in0=z_hidden[:, g], scalar1=0.0)
 
         for g in range(WHOLE_GROUPS, WHOLE_GROUPS + OUT_PASSES_BEFORE_H):
-            first_stage_passes(g, out_words[g - WHOLE_GROUPS], [OUT_BANK], stop=False)
+            first_stage_passes(g, out_words[g - WHOLE_GROUPS], OUT_BANKS, stop=False)
 
         h_grouped = keep.tile([P, HIDDEN_GROUPS, BATCH, PACK], BF16, align_bytes=64)
         h_codes = keep.tile([P, HIDDEN_GROUPS, BATCH], U32, align_bytes=64)
         h_planes = keep.tile([P, HIDDEN_GROUPS, BATCH], U8, align_bytes=64)
         for g in range(HIDDEN_GROUPS):
-            ht = work.tile([P, PACK, BATCH], BF16, tag="work")
+            zt = work.tile([P, PACK, BATCH], F32, tag="work")
             for t in range(PACK):
-                nc.tensor.transpose(ht[:, t, :], h[:, g, t, :], ident_bf16[:])
-            nc.scalar.copy(out=h_grouped[:, g], in_=ht[:].rearrange("p t b -> p b t"))
+                nc.tensor.transpose(zt[:, t, :], z_hidden[:, g, t, :], ident_f32[:])
+            nc.scalar.activation(
+                out=h_grouped[:, g], in_=zt[:].rearrange("p t b -> p b t"), func=RELU
+            )
             nc.vector.quantize_mx(
                 out=h_codes[:, g, :].bitcast(FP8X4),
                 scales=h_planes[:, g, :],
                 in_=h_grouped[:, g].rearrange("p b t -> p (b t)"),
             )
 
-        for g in range(WHOLE_GROUPS + OUT_PASSES_BEFORE_H, GROUPS - 1):
-            first_stage_passes(g, out_words[g - WHOLE_GROUPS], [OUT_BANK], stop=False)
+        for g in range(WHOLE_GROUPS + OUT_PASSES_BEFORE_H, GROUPS - OUT_PASSES_AFTER_H):
+            first_stage_passes(g, out_words[g - WHOLE_GROUPS], OUT_BANKS, stop=False)
         for g in range(HIDDEN_GROUPS):
-            nc.tensor.matmul_mx(
-                out=acc[OUT_BANK][:],
-                lhsT=h_codes[:, g, :].bitcast(FP8X4),
-                lhsT_scale=h_planes[:, g, :],
-                rhs=w1_sb[:, g, :].bitcast(FP8X4),
-                rhs_scale=w1_planes[PACK * g : P, :],
-                start=False,
-                stop=False,
-            )
-        first_stage_passes(GROUPS - 1, out_words[-1], [OUT_BANK], stop=True)
+            for i, n in enumerate(OUT_BANKS):
+                cols = slice(i * OUT_HALF, (i + 1) * OUT_HALF)
+                nc.tensor.matmul_mx(
+                    out=acc[n][:],
+                    lhsT=h_codes[:, g, :].bitcast(FP8X4),
+                    lhsT_scale=h_planes[:, g, :],
+                    rhs=w1_sb[:, g, cols].bitcast(FP8X4),
+                    rhs_scale=w1_planes[PACK * g : P, cols],
+                    start=False,
+                    stop=False,
+                )
+        for g in range(GROUPS - OUT_PASSES_AFTER_H, GROUPS):
+            first_stage_passes(g, out_words[g - WHOLE_GROUPS], OUT_BANKS, stop=(g == GROUPS - 1))
 
-        result = keep.tile([P, OUT_NODES], F32)
-        nc.vector.tensor_tensor(out=result[:], in0=acc[OUT_BANK][:], in1=bias_out[:], op=ADD)
-        nc.sync.dma_start(out=out[:, :], in_=result[:])
+        for i, queue in enumerate((nc.sync, nc.scalar)):
+            cols = slice(i * OUT_HALF, (i + 1) * OUT_HALF)
+            result = keep.tile([P, OUT_HALF], F32, name="result%d" % i)
+            nc.vector.tensor_tensor(
+                out=result[:], in0=acc[OUT_BANKS[i]][:], in1=bias_out[:, cols], op=ADD
+            )
+            queue.dma_start(out=out[:, cols], in_=result[:])

from contextlib import ExitStack

import concourse.mybir as mybir
from concourse.masks import make_identity

F32 = mybir.dt.float32
BF16 = mybir.dt.bfloat16
I32 = mybir.dt.int32
U32 = mybir.dt.uint32
U8 = mybir.dt.uint8
FP8X4 = mybir.dt.float8_e4m3fn_x4
ADD = mybir.AluOpType.add
RELU = mybir.ActivationFunctionType.Relu

P = 128
PACK = 4
K_PASS = P * PACK
N_TILE = 512

BATCH = 128
INPUTS = 16384
NODES = 1536
HIDDEN = 1024
OUT_NODES = NODES - HIDDEN
GROUPS = INPUTS // K_PASS
HIDDEN_GROUPS = HIDDEN // K_PASS
OUT_HALF = OUT_NODES // 2
OUT_BANKS = [HIDDEN_GROUPS, HIDDEN_GROUPS + 1]

QUADRANTS = 4
PLANES_PER_TILE = 4

X_CHUNK_GROUPS = 8
X_CHUNK = X_CHUNK_GROUPS * K_PASS
X_CHUNKS = GROUPS // X_CHUNK_GROUPS

SPLIT_GROUPS = 8
WHOLE_GROUPS = GROUPS - SPLIT_GROUPS
OUT_PASSES_BEFORE_H = 1
OUT_PASSES_AFTER_H = 2

FLOPS = 2 * BATCH * INPUTS * NODES + 2 * BATCH * HIDDEN * OUT_NODES


def load_scale_planes(nc, planes, scales):
    rows = PACK * scales.shape[0]
    for quadrant in range(QUADRANTS):
        nc.gpsimd.dma_start(
            out=planes[32 * quadrant : 32 * quadrant + rows, :].bitcast(F32),
            in_=scales[:, 4 * quadrant : 4 * quadrant + 4, :].bitcast(F32),
        )


def tile_spn_k_kernel(tc, x, w0_words, w0_scales, w1_words, w1_scales, biases, out):
    nc = tc.nc
    with ExitStack() as ctx:
        ctx.enter_context(tc.manual_schedule())
        keep = ctx.enter_context(tc.tile_pool(name="keep", bufs=1))
        x_pool = ctx.enter_context(tc.tile_pool(name="x", bufs=X_CHUNKS))
        stage = ctx.enter_context(tc.tile_pool(name="stage", bufs=2))
        whole_pool = ctx.enter_context(tc.tile_pool(name="whole", bufs=10))
        hidden_pool = ctx.enter_context(tc.tile_pool(name="hidden", bufs=6))
        out_pool = ctx.enter_context(tc.tile_pool(name="outcols", bufs=SPLIT_GROUPS))
        acc_pool = ctx.enter_context(tc.psum_pool(name="acc", bufs=1))
        work = ctx.enter_context(tc.psum_pool(name="work", bufs=4))

        ident_f32 = keep.tile([P, P], F32)
        make_identity(nc, ident_f32[:])

        bias_rows = keep.tile([P, NODES], BF16)
        nc.vector.memset(bias_rows[:], 0.0)
        nc.scalar.dma_start(out=bias_rows[0:1, :], in_=biases.unsqueeze(0))
        ones = keep.tile([P, P], BF16)
        nc.vector.memset(ones[:], 1.0)

        w0_planes = keep.tile([P, GROUPS // PLANES_PER_TILE, NODES], U8, align_bytes=64)
        nc.vector.memset(w0_planes[:].bitcast(I32), 0)
        w1_planes = keep.tile([P, OUT_NODES], U8, align_bytes=64)
        nc.vector.memset(w1_planes[:].bitcast(I32), 0)

        x_chunks = []
        for c in range(X_CHUNKS):
            x_chunk = x_pool.tile([P, X_CHUNK], BF16, name="x_chunk")
            nc.sync.dma_start(out=x_chunk[:], in_=x[:, c * X_CHUNK : (c + 1) * X_CHUNK])
            x_chunks.append(x_chunk)

        for c in range(GROUPS // PLANES_PER_TILE):
            load_scale_planes(
                nc, w0_planes[:, c, :], w0_scales[c * PLANES_PER_TILE : (c + 1) * PLANES_PER_TILE]
            )
        load_scale_planes(nc, w1_planes[:], w1_scales)

        x_codes = keep.tile([P, GROUPS, BATCH], U32, align_bytes=64)
        x_planes = keep.tile([P, GROUPS, BATCH], U8, align_bytes=64)
        for c in range(X_CHUNKS):
            x_words = x_chunks[c][:].bitcast(F32).rearrange("b (g p u) -> b g p u", p=P, u=2)
            grouped = stage.tile([P, X_CHUNK], BF16, align_bytes=64)
            grouped_words = grouped[:].bitcast(F32).rearrange("p (g b u) -> p g b u", b=BATCH, u=2)
            for first in range(0, X_CHUNK_GROUPS, 2):
                xt = work.tile([P, 2, 2, BATCH], F32, tag="work")
                for g in range(2):
                    for u in range(2):
                        nc.tensor.transpose(xt[:, g, u, :], x_words[:, first + g, :, u], ident_f32[:])
                nc.scalar.copy(
                    out=grouped_words[:, first : first + 2],
                    in_=xt[:].rearrange("p g u b -> p g b u"),
                )
            groups = slice(c * X_CHUNK_GROUPS, (c + 1) * X_CHUNK_GROUPS)
            nc.vector.quantize_mx(
                out=x_codes[:, groups, :].rearrange("p g b -> p (g b)").bitcast(FP8X4),
                scales=x_planes[:, groups, :].rearrange("p g b -> p (g b)"),
                in_=grouped[:],
            )

        bias_hidden = keep.tile([P, HIDDEN_GROUPS, PACK, P], F32)
        bias_out = keep.tile([P, OUT_NODES], F32)
        for n in range(NODES // N_TILE):
            spread = work.tile([P, N_TILE], F32, tag="work")
            nc.tensor.matmul(
                spread[:], lhsT=ones[:], rhs=bias_rows[:, n * N_TILE : (n + 1) * N_TILE],
                start=True, stop=True,
            )
            if n < HIDDEN_GROUPS:
                nc.vector.tensor_copy(
                    out=bias_hidden[:, n], in_=spread[:].rearrange("b (p t) -> b t p", t=PACK)
                )
            else:
                nc.vector.tensor_copy(out=bias_out[:], in_=spread[:])

        acc_nodes = [(n * N_TILE, N_TILE) for n in range(HIDDEN_GROUPS)]
        acc_nodes += [(HIDDEN + i * OUT_HALF, OUT_HALF) for i in range(2)]
        acc = [
            acc_pool.tile([P, nodes], F32, name="acc%d" % n) for n, (first, nodes) in enumerate(acc_nodes)
        ]

        def load_w0(pool, g, first_node, nodes):
            words = pool.tile([P, nodes], U32, name="words", align_bytes=64)
            nc.sync.dma_start(
                out=words[:].bitcast(I32),
                in_=w0_words[g].rearrange("p n t -> p (n t)").bitcast(I32)[
                    :, first_node : first_node + nodes
                ],
            )
            return words

        def first_stage_passes(g, words, banks, stop):
            first_word = acc_nodes[banks[0]][0]
            plane_tile, plane = divmod(g, PLANES_PER_TILE)
            for n in banks:
                first, nodes = acc_nodes[n]
                nc.tensor.matmul_mx(
                    out=acc[n][:],
                    lhsT=x_codes[:, g, :].bitcast(FP8X4),
                    lhsT_scale=x_planes[:, g, :],
                    rhs=words[:, first - first_word : first - first_word + nodes].bitcast(FP8X4),
                    rhs_scale=w0_planes[PACK * plane : P, plane_tile, first : first + nodes],
                    start=(g == 0),
                    stop=stop,
                )

        hidden_banks = list(range(HIDDEN_GROUPS))
        for g in range(WHOLE_GROUPS):
            words = load_w0(whole_pool, g, 0, NODES)
            first_stage_passes(g, words, hidden_banks + OUT_BANKS, stop=False)
        for g in range(WHOLE_GROUPS, GROUPS):
            words = load_w0(hidden_pool, g, 0, HIDDEN)
            first_stage_passes(g, words, hidden_banks, stop=(g == GROUPS - 1))
        w1_sb = keep.tile([P, HIDDEN_GROUPS, OUT_NODES], U32, align_bytes=64)
        nc.sync.dma_start(
            out=w1_sb[:].bitcast(I32),
            in_=w1_words.rearrange("g p n t -> p g (n t)").bitcast(I32),
        )
        out_words = [load_w0(out_pool, g, HIDDEN, OUT_NODES) for g in range(WHOLE_GROUPS, GROUPS)]

        z_hidden = keep.tile([P, HIDDEN_GROUPS, PACK, P], F32)
        for g in range(HIDDEN_GROUPS):
            nc.vector.tensor_tensor(
                out=z_hidden[:, g],
                in0=acc[g][:].rearrange("b (p t) -> b t p", t=PACK),
                in1=bias_hidden[:, g],
                op=ADD,
            )

        for g in range(WHOLE_GROUPS, WHOLE_GROUPS + OUT_PASSES_BEFORE_H):
            first_stage_passes(g, out_words[g - WHOLE_GROUPS], OUT_BANKS, stop=False)

        h_grouped = keep.tile([P, HIDDEN_GROUPS, BATCH, PACK], BF16, align_bytes=64)
        h_codes = keep.tile([P, HIDDEN_GROUPS, BATCH], U32, align_bytes=64)
        h_planes = keep.tile([P, HIDDEN_GROUPS, BATCH], U8, align_bytes=64)
        for g in range(HIDDEN_GROUPS):
            zt = work.tile([P, PACK, BATCH], F32, tag="work")
            for t in range(PACK):
                nc.tensor.transpose(zt[:, t, :], z_hidden[:, g, t, :], ident_f32[:])
            nc.scalar.activation(
                out=h_grouped[:, g], in_=zt[:].rearrange("p t b -> p b t"), func=RELU
            )
            nc.vector.quantize_mx(
                out=h_codes[:, g, :].bitcast(FP8X4),
                scales=h_planes[:, g, :],
                in_=h_grouped[:, g].rearrange("p b t -> p (b t)"),
            )

        for g in range(WHOLE_GROUPS + OUT_PASSES_BEFORE_H, GROUPS - OUT_PASSES_AFTER_H):
            first_stage_passes(g, out_words[g - WHOLE_GROUPS], OUT_BANKS, stop=False)
        for g in range(HIDDEN_GROUPS):
            for i, n in enumerate(OUT_BANKS):
                cols = slice(i * OUT_HALF, (i + 1) * OUT_HALF)
                nc.tensor.matmul_mx(
                    out=acc[n][:],
                    lhsT=h_codes[:, g, :].bitcast(FP8X4),
                    lhsT_scale=h_planes[:, g, :],
                    rhs=w1_sb[:, g, cols].bitcast(FP8X4),
                    rhs_scale=w1_planes[PACK * g : P, cols],
                    start=False,
                    stop=False,
                )
        for g in range(GROUPS - OUT_PASSES_AFTER_H, GROUPS):
            first_stage_passes(g, out_words[g - WHOLE_GROUPS], OUT_BANKS, stop=(g == GROUPS - 1))

        for i, queue in enumerate((nc.sync, nc.scalar)):
            cols = slice(i * OUT_HALF, (i + 1) * OUT_HALF)
            result = keep.tile([P, OUT_HALF], F32, name="result%d" % i)
            nc.vector.tensor_tensor(
                out=result[:], in0=acc[OUT_BANKS[i]][:], in1=bias_out[:, cols], op=ADD
            )
            queue.dma_start(out=out[:, cols], in_=result[:])
